import numpy as np
import ml_dtypes


def mxq(x, axis, fmt="e4m3"):
    dtype, down = {"e4m3": (ml_dtypes.float8_e4m3fn, 7), "e5m2": (ml_dtypes.float8_e5m2, 14)}[fmt]
    v = np.moveaxis(np.asarray(x, np.float32).astype(ml_dtypes.bfloat16).astype(np.float64), axis, -1)
    blocks = v.reshape(v.shape[:-1] + (-1, 32))
    amax = np.abs(blocks).max(-1, keepdims=True)
    byte = np.maximum(np.where(amax > 0, np.frexp(amax)[1] - 1 + 127, 0) - down, 1)
    scale = np.exp2(byte - 127.0)
    codes = (blocks / scale).astype(np.float32).astype(dtype).astype(np.float64)
    return np.moveaxis((codes * scale).reshape(v.shape), -1, axis)


WIDE = False


def mx_kscale(k):
    if not WIDE:
        return np.ones(k)
    levels = np.array([10, -10, 5, -5, 0])
    a = np.random.permutation(np.resize(levels, k // 512 * 4)).reshape(k // 512, 4)
    idx = np.arange(k)
    return np.exp2(a[idx // 512, idx % 128 // 32])


BF16 = ml_dtypes.bfloat16


def bf(x):
    return np.asarray(x, np.float32).astype(BF16)


def f64(x):
    return np.asarray(x).astype(np.float64)


E2M1 = np.array([0.0, 0.5, 1.0, 1.5, 2.0, 3.0, 4.0, 6.0, -0.0, -0.5, -1.0, -1.5, -2.0, -3.0, -4.0, -6.0])


def pack_weight(w, fmt):
    k, n = w.shape
    w = f64(bf(w)).reshape(k // 32, 32, n)
    amax = np.abs(w).max(1)
    if fmt == "e4m3":
        byte = np.frexp(amax)[1] - 1 + 127 - 7
    else:
        mant, ex = np.frexp(amax / 6.0)
        byte = np.where(mant > 0.5, ex, ex - 1) + 127
    byte = np.clip(np.where(amax > 0, byte, 1), 1, 254)
    scaled = (w * np.exp2(127.0 - byte)[:, None, :]).reshape(k, n).astype(np.float32)
    by_word = np.ascontiguousarray(scaled.reshape(k // 512, 128, 4, n).transpose(0, 1, 3, 2))
    if fmt == "e4m3":
        words = by_word.astype(ml_dtypes.float8_e4m3fn).view(np.uint8)
    else:
        c = by_word.astype(ml_dtypes.float4_e2m1fn).view(np.uint8) & 0xF
        words = c[..., 0::2] | (c[..., 1::2] << 4)
    return np.ascontiguousarray(words), np.ascontiguousarray(byte.astype(np.uint8).reshape(k // 512, 16, n))


def unpack_weight(words, scales, fmt):
    g, p, n, _ = words.shape
    if fmt == "e4m3":
        vals = np.ascontiguousarray(words).view(ml_dtypes.float8_e4m3fn).astype(np.float64)
    else:
        nib = np.empty((g, p, n, 4), np.uint8)
        nib[..., 0::2] = words & 0xF
        nib[..., 1::2] = words >> 4
        vals = E2M1[nib]
    vals = vals * np.repeat(np.exp2(scales.astype(np.float64) - 127.0), 8, axis=1)[..., None]
    return vals.transpose(0, 1, 3, 2).reshape(g * 512, n)


B, T, STOCH, ACT, HID, DETER, G = 4, 64, 1024, 512, 512, 4096, 8
N = B * T
BH = DETER // G


def silu(v):
    return v / (1.0 + np.exp(-v))


def sigmoid(v):
    return 1.0 / (1.0 + np.exp(-v))


def setup_inputs():
    t = mx_kscale(DETER)
    h = bf(silu(np.random.standard_normal((N, DETER))) * t)
    d = bf(np.random.standard_normal((B, T, DETER)))
    stack = np.random.standard_normal((G, BH, 3 * BH)) * 2.0 / np.sqrt(BH) / t.reshape(G, BH)[:, :, None]
    words, scales = pack_weight(stack.reshape(-1, 3 * BH), "e4m3")
    b_gate = bf(0.3 * np.random.standard_normal((G, 3 * BH)))
    return {
        "h": h,
        "d": d,
        "W_gate_words": words,
        "W_gate_scales": scales,
        "b_gate": b_gate,
    }


def reference(h, d, W_gate_words, W_gate_scales, b_gate):
    hq = mxq(f64(h).reshape(N, G, BH).transpose(1, 0, 2), 2, "e4m3")
    wq = unpack_weight(W_gate_words, W_gate_scales, "e4m3").reshape(G, BH, 3 * BH)
    gates = (hq @ wq) + f64(b_gate)[:, None, :]
    gates = gates.transpose(1, 0, 2)
    reset, update, cand = np.split(gates, 3, axis=-1)
    reset = sigmoid(reset.reshape(N, DETER))
    update = sigmoid(update.reshape(N, DETER) - 1.0)
    cand = np.tanh(reset * cand.reshape(N, DETER))
    d2 = f64(d).reshape(N, DETER)
    return (update * cand + (1.0 - update) * d2).reshape(B, T, DETER)

@@ -1,0 +1,274 @@
+from contextlib import ExitStack
+
+import concourse.mybir as mybir
+from concourse.masks import make_identity
+
+F32 = mybir.dt.float32
+BF16 = mybir.dt.bfloat16
+I32 = mybir.dt.int32
+U32 = mybir.dt.uint32
+U8 = mybir.dt.uint8
+FP8X4 = mybir.dt.float8_e4m3fn_x4
+ACT = mybir.ActivationFunctionType
+ALU = mybir.AluOpType
+
+P = 128
+ROWS = 256
+ROW_TILES = ROWS // P
+GROUPS = 8
+BLOCK = 512
+GATES = 3
+R_GATE = 0
+U_GATE = 1
+C_GATE = 2
+FEATURE_TILES = BLOCK // P
+HALVES = 2
+TILES_PER_HALF = FEATURE_TILES // HALVES
+HALF = BLOCK // HALVES
+GROUPS_PER_H_LOAD = 2
+GROUPS_PER_D_LOAD = 2
+PLANES_PER_TILE = 4
+BIAS_ROWS = GROUPS * GATES * FEATURE_TILES
+
+FLOPS = 2 * ROWS * BLOCK * GATES * BLOCK * GROUPS
+
+
+def tile_blockrecurrentmodel_pb_e_kernel(tc, h, d, W_gate_words, W_gate_scales, b_gate, out):
+    nc = tc.nc
+    h_rows = h.rearrange("(m p) k -> p m k", p=P)
+    d_rows = d.rearrange("b t k -> (b t) k").rearrange("(m p) k -> p m k", p=P)
+    out_rows = out.rearrange("b t k -> (b t) k").rearrange("(m p) k -> p m k", p=P)
+
+    with ExitStack() as ctx:
+        ctx.enter_context(tc.manual_schedule())
+        consts = ctx.enter_context(tc.tile_pool(name="consts", bufs=1))
+        resident = ctx.enter_context(tc.tile_pool(name="resident", bufs=1))
+        stage = ctx.enter_context(tc.tile_pool(name="stage", bufs=2))
+        work = ctx.enter_context(tc.tile_pool(name="work", bufs=2))
+
+        ident_f32 = consts.tile([P, P], F32)
+        make_identity(nc, ident_f32[:])
+        ident_bf16 = consts.tile([P, P], BF16)
+        make_identity(nc, ident_bf16[:])
+
+        bias_rows = consts.tile([P, P], BF16)
+        nc.vector.memset(bias_rows[:], 0.0)
+        nc.scalar.dma_start(out=bias_rows[0:BIAS_ROWS, :], in_=b_gate.rearrange("g (c p) -> (g c) p", p=P))
+
+        warm = consts.tile([P, 1], F32)
+        nc.vector.memset(warm[:], 0.0)
+        nc.scalar.activation(out=warm[:], in_=warm[:], func=ACT.Sigmoid)
+
+        h_sb = []
+        for c in range(GROUPS // GROUPS_PER_H_LOAD):
+            cols = slice(c * GROUPS_PER_H_LOAD * BLOCK, (c + 1) * GROUPS_PER_H_LOAD * BLOCK)
+            h_chunk = resident.tile([P, ROW_TILES, GROUPS_PER_H_LOAD * BLOCK], BF16, name="h_chunk%d" % c)
+            nc.sync.dma_start(out=h_chunk[:], in_=h_rows[:, :, cols])
+            h_sb.append(h_chunk)
+
+        w_scales = consts.tile([P, GROUPS // PLANES_PER_TILE, GATES * BLOCK], U8, align_bytes=64)
+        nc.vector.memset(w_scales[:].rearrange("p a n -> p (a n)").bitcast(I32), 0)
+        for a in range(GROUPS // PLANES_PER_TILE):
+            for quadrant in range(4):
+                nc.sync.dma_start(
+                    out=w_scales[32 * quadrant : 32 * quadrant + 16, a, :].bitcast(I32),
+                    in_=W_gate_scales[
+                        PLANES_PER_TILE * a : PLANES_PER_TILE * (a + 1), 4 * quadrant : 4 * quadrant + 4, :
+                    ].bitcast(I32),
+                )
+
+        w_words = []
+        d_sb = []
+        for g in range(GROUPS):
+            words = resident.tile([P, GATES * BLOCK], U32, name="w_words%d" % g, align_bytes=64)
+            nc.sync.dma_start(
+                out=words[:].bitcast(I32),
+                in_=W_gate_words[g].rearrange("p n t -> p (n t)").bitcast(I32),
+            )
+            w_words.append(words)
+            if g % GROUPS_PER_D_LOAD == GROUPS_PER_D_LOAD - 1:
+                c = g // GROUPS_PER_D_LOAD
+                cols = slice(c * GROUPS_PER_D_LOAD * BLOCK, (c + 1) * GROUPS_PER_D_LOAD * BLOCK)
+                d_chunk = resident.tile([P, ROW_TILES, GROUPS_PER_D_LOAD * BLOCK], BF16, name="d_chunk%d" % c)
+                nc.sync.dma_start(out=d_chunk[:], in_=d_rows[:, :, cols])
+                d_sb.append(d_chunk)
+
+        def d_block(g, first_feature, features):
+            start = (g % GROUPS_PER_D_LOAD) * BLOCK + first_feature
+            return d_sb[g // GROUPS_PER_D_LOAD][:, :, start : start + features]
+
+        h_codes = consts.tile([P, GROUPS, ROWS], U32, align_bytes=64)
+        h_scales = consts.tile([P, GROUPS, ROWS], U8, align_bytes=64)
+        bias = consts.tile([P, P], F32)
+
+        def bias_column(g, gate, j):
+            column = (g * GATES + gate) * FEATURE_TILES + j
+            return bias[:, column : column + 1]
+
+        with tc.psum_pool(name="prologue_psum", bufs=1) as prologue_psum:
+            for g in range(GROUPS):
+                h_t = prologue_psum.tile([P, 2, ROWS], F32, bufs=4)
+                first_word = (g % GROUPS_PER_H_LOAD) * (BLOCK // 2)
+                for m in range(ROW_TILES):
+                    h_words = h_sb[g // GROUPS_PER_H_LOAD][:, m, :].bitcast(F32)
+                    for u in range(2):
+                        nc.tensor.transpose(
+                            h_t[:, u, m * P : (m + 1) * P],
+                            h_words[:, first_word + u : first_word + BLOCK // 2 : 2],
+                            ident_f32[:],
+                        )
+                grouped = stage.tile([P, ROWS * 4], BF16, align_bytes=64, bufs=4)
+                nc.scalar.copy(
+                    out=grouped[:].bitcast(F32).rearrange("p (n u) -> p n u", u=2),
+                    in_=h_t[:].rearrange("p u n -> p n u"),
+                )
+                nc.vector.quantize_mx(
+                    out=h_codes[:, g, :].bitcast(FP8X4), scales=h_scales[:, g, :], in_=grouped[:]
+                )
+
+            bias_ps = prologue_psum.tile([P, P], BF16)
+            nc.tensor.transpose(bias_ps[:], bias_rows[:], ident_bf16[:])
+            nc.vector.tensor_copy(out=bias[:], in_=bias_ps[:])
+            u_bias = bias[:, 0:BIAS_ROWS].rearrange("p (g c) -> p g c", c=GATES * FEATURE_TILES)[
+                :, :, U_GATE * FEATURE_TILES : (U_GATE + 1) * FEATURE_TILES
+            ]
+            nc.vector.tensor_scalar_add(out=u_bias, in0=u_bias, scalar1=-1.0)
+
+        psum = ctx.enter_context(tc.psum_pool(name="psum", bufs=1))
+        gate_ps = {}
+        reset = {}
+        update = {}
+        cand_in = {}
+        cand = {}
+        d_t = {}
+        diff = {}
+        step = {}
+        step_t = {}
+        result = {}
+
+        def project(g):
+            offset = 4 * (g % PLANES_PER_TILE)
+            for gate, tag in ((R_GATE, "r_ps"), (C_GATE, "c_ps"), (U_GATE, "u_ps")):
+                for half in range(HALVES):
+                    bank = psum.tile([P, TILES_PER_HALF, ROWS], F32, name=tag, tag=tag, bufs=HALVES)
+                    gate_ps[(g, gate, half)] = bank
+                    for i in range(TILES_PER_HALF):
+                        first = gate * BLOCK + (half * TILES_PER_HALF + i) * P
+                        nc.tensor.matmul_mx(
+                            out=bank[:, i, :],
+                            lhsT=w_words[g][:, first : first + P].bitcast(FP8X4),
+                            lhsT_scale=w_scales[offset:P, g // PLANES_PER_TILE, first : first + P],
+                            rhs=h_codes[:, g, :].bitcast(FP8X4),
+                            rhs_scale=h_scales[:, g, :],
+                            start=True,
+                            stop=True,
+                        )
+
+        def sigmoid_gate(g, gate, target):
+            target[g] = work.tile([P, FEATURE_TILES, ROWS], F32, name="sig%d" % gate, tag="sig%d" % gate, bufs=3)
+            for j in range(FEATURE_TILES):
+                nc.scalar.activation(
+                    out=target[g][:, j, :],
+                    in_=gate_ps[(g, gate, j // TILES_PER_HALF)][:, j % TILES_PER_HALF, :],
+                    func=ACT.Sigmoid,
+                    bias=bias_column(g, gate, j),
+                    scale=1.0,
+                )
+
+        def candidate_input(g, half):
+            if half == 0:
+                cand_in[g] = work.tile([P, FEATURE_TILES, ROWS], F32, name="cand_in", tag="cand_in")
+            for i in range(TILES_PER_HALF):
+                j = half * TILES_PER_HALF + i
+                nc.vector.scalar_tensor_tensor(
+                    out=cand_in[g][:, j, :],
+                    in0=gate_ps[(g, C_GATE, half)][:, i, :],
+                    scalar=bias_column(g, C_GATE, j),
+                    in1=reset[g][:, j, :],
+                    op0=ALU.add,
+                    op1=ALU.mult,
+                )
+
+        def half_tiles(half):
+            return slice(half * TILES_PER_HALF, (half + 1) * TILES_PER_HALF)
+
+        def candidate(g):
+            cand[g] = work.tile([P, FEATURE_TILES, ROWS], F32, name="cand", tag="cand")
+            for half in range(HALVES):
+                nc.scalar.activation(
+                    out=cand[g][:, half_tiles(half), :], in_=cand_in[g][:, half_tiles(half), :], func=ACT.Tanh
+                )
+
+        def transpose_d(g):
+            d_t[g] = psum.tile([P, FEATURE_TILES, ROWS], BF16, name="d_t", tag="d_t")
+            for j in range(FEATURE_TILES):
+                for m in range(ROW_TILES):
+                    nc.tensor.transpose(
+                        d_t[g][:, j, m * P : (m + 1) * P], d_block(g, j * P, P)[:, m, :], ident_bf16[:]
+                    )
+
+        def blend(g):
+            diff[g] = work.tile([P, FEATURE_TILES, ROWS], F32, name="diff", tag="diff")
+            step[g] = work.tile([P, FEATURE_TILES, ROWS], F32, name="step", tag="step", bufs=3)
+            for half in range(HALVES):
+                nc.vector.tensor_tensor(
+                    out=diff[g][:, half_tiles(half), :],
+                    in0=cand[g][:, half_tiles(half), :],
+                    in1=d_t[g][:, half_tiles(half), :],
+                    op=ALU.subtract,
+                )
+            for half in range(HALVES):
+                nc.gpsimd.tensor_tensor(
+                    out=step[g][:, half_tiles(half), :],
+                    in0=diff[g][:, half_tiles(half), :],
+                    in1=update[g][:, half_tiles(half), :],
+                    op=ALU.mult,
+                )
+
+        def transpose_step(g, half):
+            step_t[(g, half)] = psum.tile([P, ROW_TILES, HALF], F32, name="step_t", tag="step_t")
+            for m in range(ROW_TILES):
+                for i in range(TILES_PER_HALF):
+                    nc.tensor.transpose(
+                        step_t[(g, half)][:, m, i * P : (i + 1) * P],
+                        step[g][:, half * TILES_PER_HALF + i, m * P : (m + 1) * P],
+                        ident_f32[:],
+                    )
+
+        def finish(g, half):
+            if half == 0:
+                result[g] = work.tile([P, ROW_TILES, BLOCK], F32, name="result", tag="result", bufs=3)
+            nc.vector.tensor_tensor(
+                out=result[g][:, :, half * HALF : (half + 1) * HALF],
+                in0=step_t[(g, half)][:],
+                in1=d_block(g, half * HALF, HALF),
+                op=ALU.add,
+            )
+            if half == HALVES - 1:
+                nc.sync.dma_start(out=out_rows[:, :, g * BLOCK : (g + 1) * BLOCK], in_=result[g][:])
+
+        def is_group(g):
+            return 0 <= g < GROUPS
+
+        for i in range(-1, GROUPS + 3):
+            if is_group(i - 3):
+                finish(i - 3, 0)
+                transpose_step(i - 3, 1)
+            if is_group(i):
+                sigmoid_gate(i, R_GATE, reset)
+                candidate_input(i, 0)
+            if is_group(i - 3):
+                finish(i - 3, 1)
+            if is_group(i - 1):
+                transpose_d(i - 1)
+            if is_group(i - 2):
+                transpose_step(i - 2, 0)
+            if is_group(i):
+                candidate_input(i, 1)
+            if is_group(i - 1):
+                candidate(i - 1)
+                blend(i - 1)
+            if is_group(i):
+                sigmoid_gate(i, U_GATE, update)
+            if is_group(i + 1):
+                project(i + 1)

@@ -22,9 +22,10 @@ R_GATE = 0
 U_GATE = 1
 C_GATE = 2
 FEATURE_TILES = BLOCK // P
-HALVES = 2
-TILES_PER_HALF = FEATURE_TILES // HALVES
-HALF = BLOCK // HALVES
+UNIT_TILES = 2
+UNIT = UNIT_TILES * P
+UNITS_PER_GROUP = BLOCK // UNIT
+UNITS = GROUPS * UNITS_PER_GROUP
 GROUPS_PER_H_LOAD = 2
 GROUPS_PER_D_LOAD = 2
 PLANES_PER_TILE = 4
@@ -68,7 +69,8 @@ def tile_blockrecurrentmodel_pb_e_kernel(tc, h, d, W_gate_words, W_gate_scales, 
 
         w_scales = consts.tile([P, GROUPS // PLANES_PER_TILE, GATES * BLOCK], U8, align_bytes=64)
         nc.vector.memset(w_scales[:].rearrange("p a n -> p (a n)").bitcast(I32), 0)
-        for a in range(GROUPS // PLANES_PER_TILE):
+
+        def load_scales(a):
             for quadrant in range(4):
                 nc.sync.dma_start(
                     out=w_scales[32 * quadrant : 32 * quadrant + 16, a, :].bitcast(I32),
@@ -80,6 +82,8 @@ def tile_blockrecurrentmodel_pb_e_kernel(tc, h, d, W_gate_words, W_gate_scales, 
         w_words = []
         d_sb = []
         for g in range(GROUPS):
+            if g % PLANES_PER_TILE == 0:
+                load_scales(g // PLANES_PER_TILE)
             words = resident.tile([P, GATES * BLOCK], U32, name="w_words%d" % g, align_bytes=64)
             nc.sync.dma_start(
                 out=words[:].bitcast(I32),
@@ -135,6 +139,7 @@ def tile_blockrecurrentmodel_pb_e_kernel(tc, h, d, W_gate_words, W_gate_scales, 
             nc.vector.tensor_scalar_add(out=u_bias, in0=u_bias, scalar1=-1.0)
 
         psum = ctx.enter_context(tc.psum_pool(name="psum", bufs=1))
+        unit_shape = [P, UNIT_TILES, ROWS]
         gate_ps = {}
         reset = {}
         update = {}
@@ -144,131 +149,104 @@ def tile_blockrecurrentmodel_pb_e_kernel(tc, h, d, W_gate_words, W_gate_scales, 
         diff = {}
         step = {}
         step_t = {}
-        result = {}
 
-        def project(g):
+        def project(k):
+            g = k // UNITS_PER_GROUP
             offset = 4 * (g % PLANES_PER_TILE)
             for gate, tag in ((R_GATE, "r_ps"), (C_GATE, "c_ps"), (U_GATE, "u_ps")):
-                for half in range(HALVES):
-                    bank = psum.tile([P, TILES_PER_HALF, ROWS], F32, name=tag, tag=tag, bufs=HALVES)
-                    gate_ps[(g, gate, half)] = bank
-                    for i in range(TILES_PER_HALF):
-                        first = gate * BLOCK + (half * TILES_PER_HALF + i) * P
-                        nc.tensor.matmul_mx(
-                            out=bank[:, i, :],
-                            lhsT=w_words[g][:, first : first + P].bitcast(FP8X4),
-                            lhsT_scale=w_scales[offset:P, g // PLANES_PER_TILE, first : first + P],
-                            rhs=h_codes[:, g, :].bitcast(FP8X4),
-                            rhs_scale=h_scales[:, g, :],
-                            start=True,
-                            stop=True,
-                        )
+                bank = psum.tile(unit_shape, F32, name=tag, tag=tag, bufs=2)
+                gate_ps[(k, gate)] = bank
+                for i in range(UNIT_TILES):
+                    first = gate * BLOCK + (k % UNITS_PER_GROUP) * UNIT + i * P
+                    nc.tensor.matmul_mx(
+                        out=bank[:, i, :],
+                        lhsT=w_words[g][:, first : first + P].bitcast(FP8X4),
+                        lhsT_scale=w_scales[offset:P, g // PLANES_PER_TILE, first : first + P],
+                        rhs=h_codes[:, g, :].bitcast(FP8X4),
+                        rhs_scale=h_scales[:, g, :],
+                        start=True,
+                        stop=True,
+                    )
 
-        def sigmoid_gate(g, gate, target):
-            target[g] = work.tile([P, FEATURE_TILES, ROWS], F32, name="sig%d" % gate, tag="sig%d" % gate, bufs=3)
-            for j in range(FEATURE_TILES):
+        def unit_bias(k, gate, i):
+            return bias_column(k // UNITS_PER_GROUP, gate, (k % UNITS_PER_GROUP) * UNIT_TILES + i)
+
+        def sigmoid_gate(k, gate, target, tag):
+            target[k] = work.tile(unit_shape, F32, name=tag, tag=tag, bufs=3)
+            for i in range(UNIT_TILES):
                 nc.scalar.activation(
-                    out=target[g][:, j, :],
-                    in_=gate_ps[(g, gate, j // TILES_PER_HALF)][:, j % TILES_PER_HALF, :],
+                    out=target[k][:, i, :],
+                    in_=gate_ps[(k, gate)][:, i, :],
                     func=ACT.Sigmoid,
-                    bias=bias_column(g, gate, j),
+                    bias=unit_bias(k, gate, i),
                     scale=1.0,
                 )
 
-        def candidate_input(g, half):
-            if half == 0:
-                cand_in[g] = work.tile([P, FEATURE_TILES, ROWS], F32, name="cand_in", tag="cand_in")
-            for i in range(TILES_PER_HALF):
-                j = half * TILES_PER_HALF + i
+        def candidate_input(k):
+            cand_in[k] = work.tile(unit_shape, F32, name="cand_in", tag="cand_in", bufs=3)
+            for i in range(UNIT_TILES):
                 nc.vector.scalar_tensor_tensor(
-                    out=cand_in[g][:, j, :],
-                    in0=gate_ps[(g, C_GATE, half)][:, i, :],
-                    scalar=bias_column(g, C_GATE, j),
-                    in1=reset[g][:, j, :],
+                    out=cand_in[k][:, i, :],
+                    in0=gate_ps[(k, C_GATE)][:, i, :],
+                    scalar=unit_bias(k, C_GATE, i),
+                    in1=reset[k][:, i, :],
                     op0=ALU.add,
                     op1=ALU.mult,
                 )
 
-        def half_tiles(half):
-            return slice(half * TILES_PER_HALF, (half + 1) * TILES_PER_HALF)
+        def candidate(k):
+            cand[k] = work.tile(unit_shape, F32, name="cand", tag="cand", bufs=2)
+            nc.scalar.activation(out=cand[k][:], in_=cand_in[k][:], func=ACT.Tanh)
 
-        def candidate(g):
-            cand[g] = work.tile([P, FEATURE_TILES, ROWS], F32, name="cand", tag="cand")
-            for half in range(HALVES):
-                nc.scalar.activation(
-                    out=cand[g][:, half_tiles(half), :], in_=cand_in[g][:, half_tiles(half), :], func=ACT.Tanh
-                )
+        def d_unit(k, first_feature, features):
+            return d_block(k // UNITS_PER_GROUP, (k % UNITS_PER_GROUP) * UNIT + first_feature, features)
 
-        def transpose_d(g):
-            d_t[g] = psum.tile([P, FEATURE_TILES, ROWS], BF16, name="d_t", tag="d_t")
-            for j in range(FEATURE_TILES):
+        def transpose_d(k):
+            d_t[k] = psum.tile(unit_shape, BF16, name="d_t", tag="d_t")
+            for i in range(UNIT_TILES):
                 for m in range(ROW_TILES):
-                    nc.tensor.transpose(
-                        d_t[g][:, j, m * P : (m + 1) * P], d_block(g, j * P, P)[:, m, :], ident_bf16[:]
-                    )
+                    nc.tensor.transpose(d_t[k][:, i, m * P : (m + 1) * P], d_unit(k, i * P, P)[:, m, :], ident_bf16[:])
 
-        def blend(g):
-            diff[g] = work.tile([P, FEATURE_TILES, ROWS], F32, name="diff", tag="diff")
-            step[g] = work.tile([P, FEATURE_TILES, ROWS], F32, name="step", tag="step", bufs=3)
-            for half in range(HALVES):
-                nc.vector.tensor_tensor(
-                    out=diff[g][:, half_tiles(half), :],
-                    in0=cand[g][:, half_tiles(half), :],
-                    in1=d_t[g][:, half_tiles(half), :],
-                    op=ALU.subtract,
-                )
-            for half in range(HALVES):
-                nc.gpsimd.tensor_tensor(
-                    out=step[g][:, half_tiles(half), :],
-                    in0=diff[g][:, half_tiles(half), :],
-                    in1=update[g][:, half_tiles(half), :],
-                    op=ALU.mult,
-                )
+        def difference(k):
+            diff[k] = work.tile(unit_shape, F32, name="diff", tag="diff", bufs=2)
+            nc.vector.tensor_tensor(out=diff[k][:], in0=cand[k][:], in1=d_t[k][:], op=ALU.subtract)
 
-        def transpose_step(g, half):
-            step_t[(g, half)] = psum.tile([P, ROW_TILES, HALF], F32, name="step_t", tag="step_t")
+        def scale_by_update(k):
+            step[k] = work.tile(unit_shape, F32, name="step", tag="step", bufs=3)
+            nc.gpsimd.tensor_tensor(out=step[k][:], in0=diff[k][:], in1=update[k][:], op=ALU.mult)
+
+        def transpose_step(k):
+            step_t[k] = psum.tile([P, ROW_TILES, UNIT], F32, name="step_t", tag="step_t")
             for m in range(ROW_TILES):
-                for i in range(TILES_PER_HALF):
+                for i in range(UNIT_TILES):
                     nc.tensor.transpose(
-                        step_t[(g, half)][:, m, i * P : (i + 1) * P],
-                        step[g][:, half * TILES_PER_HALF + i, m * P : (m + 1) * P],
-                        ident_f32[:],
+                        step_t[k][:, m, i * P : (i + 1) * P], step[k][:, i, m * P : (m + 1) * P], ident_f32[:]
                     )
 
-        def finish(g, half):
-            if half == 0:
-                result[g] = work.tile([P, ROW_TILES, BLOCK], F32, name="result", tag="result", bufs=3)
-            nc.vector.tensor_tensor(
-                out=result[g][:, :, half * HALF : (half + 1) * HALF],
-                in0=step_t[(g, half)][:],
-                in1=d_block(g, half * HALF, HALF),
-                op=ALU.add,
-            )
-            if half == HALVES - 1:
-                nc.sync.dma_start(out=out_rows[:, :, g * BLOCK : (g + 1) * BLOCK], in_=result[g][:])
+        def finish(k):
+            result = work.tile([P, ROW_TILES, UNIT], F32, bufs=4)
+            nc.vector.tensor_tensor(out=result[:], in0=step_t[k][:], in1=d_unit(k, 0, UNIT), op=ALU.add)
+            nc.sync.dma_start(out=out_rows[:, :, k * UNIT : (k + 1) * UNIT], in_=result[:])
 
-        def is_group(g):
-            return 0 <= g < GROUPS
+        def is_unit(k):
+            return 0 <= k < UNITS
 
-        for i in range(-1, GROUPS + 3):
-            if is_group(i - 3):
-                finish(i - 3, 0)
-                transpose_step(i - 3, 1)
-            if is_group(i):
-                sigmoid_gate(i, R_GATE, reset)
-                candidate_input(i, 0)
-            if is_group(i - 3):
-                finish(i - 3, 1)
-            if is_group(i - 1):
-                transpose_d(i - 1)
-            if is_group(i - 2):
-                transpose_step(i - 2, 0)
-            if is_group(i):
-                candidate_input(i, 1)
-            if is_group(i - 1):
-                candidate(i - 1)
-                blend(i - 1)
-            if is_group(i):
-                sigmoid_gate(i, U_GATE, update)
-            if is_group(i + 1):
-                project(i + 1)
+        project(0)
+        for k in range(UNITS + 3):
+            if is_unit(k - 3):
+                finish(k - 3)
+            if is_unit(k - 1):
+                transpose_d(k - 1)
+            if is_unit(k):
+                sigmoid_gate(k, R_GATE, reset, "reset")
+                candidate_input(k)
+            if is_unit(k + 1):
+                project(k + 1)
+            if is_unit(k - 1):
+                candidate(k - 1)
+                difference(k - 1)
+                scale_by_update(k - 1)
+            if is_unit(k - 2):
+                transpose_step(k - 2)
+            if is_unit(k):
+                sigmoid_gate(k, U_GATE, update, "update")

@@ -150,23 +150,22 @@ def tile_blockrecurrentmodel_pb_e_kernel(tc, h, d, W_gate_words, W_gate_scales, 
         step = {}
         step_t = {}
 
-        def project(k):
+        def project(k, gate, tag, banks):
             g = k // UNITS_PER_GROUP
             offset = 4 * (g % PLANES_PER_TILE)
-            for gate, tag in ((R_GATE, "r_ps"), (C_GATE, "c_ps"), (U_GATE, "u_ps")):
-                bank = psum.tile(unit_shape, F32, name=tag, tag=tag, bufs=2)
-                gate_ps[(k, gate)] = bank
-                for i in range(UNIT_TILES):
-                    first = gate * BLOCK + (k % UNITS_PER_GROUP) * UNIT + i * P
-                    nc.tensor.matmul_mx(
-                        out=bank[:, i, :],
-                        lhsT=w_words[g][:, first : first + P].bitcast(FP8X4),
-                        lhsT_scale=w_scales[offset:P, g // PLANES_PER_TILE, first : first + P],
-                        rhs=h_codes[:, g, :].bitcast(FP8X4),
-                        rhs_scale=h_scales[:, g, :],
-                        start=True,
-                        stop=True,
-                    )
+            bank = psum.tile(unit_shape, F32, name=tag, tag=tag, bufs=banks)
+            gate_ps[(k, gate)] = bank
+            for i in range(UNIT_TILES):
+                first = gate * BLOCK + (k % UNITS_PER_GROUP) * UNIT + i * P
+                nc.tensor.matmul_mx(
+                    out=bank[:, i, :],
+                    lhsT=w_words[g][:, first : first + P].bitcast(FP8X4),
+                    lhsT_scale=w_scales[offset:P, g // PLANES_PER_TILE, first : first + P],
+                    rhs=h_codes[:, g, :].bitcast(FP8X4),
+                    rhs_scale=h_scales[:, g, :],
+                    start=True,
+                    stop=True,
+                )
 
         def unit_bias(k, gate, i):
             return bias_column(k // UNITS_PER_GROUP, gate, (k % UNITS_PER_GROUP) * UNIT_TILES + i)
@@ -216,7 +215,7 @@ def tile_blockrecurrentmodel_pb_e_kernel(tc, h, d, W_gate_words, W_gate_scales, 
             nc.gpsimd.tensor_tensor(out=step[k][:], in0=diff[k][:], in1=update[k][:], op=ALU.mult)
 
         def transpose_step(k):
-            step_t[k] = psum.tile([P, ROW_TILES, UNIT], F32, name="step_t", tag="step_t")
+            step_t[k] = psum.tile([P, ROW_TILES, UNIT], F32, name="step_t", tag="step_t", bufs=2)
             for m in range(ROW_TILES):
                 for i in range(UNIT_TILES):
                     nc.tensor.transpose(
@@ -231,22 +230,24 @@ def tile_blockrecurrentmodel_pb_e_kernel(tc, h, d, W_gate_words, W_gate_scales, 
         def is_unit(k):
             return 0 <= k < UNITS
 
-        project(0)
-        for k in range(UNITS + 3):
-            if is_unit(k - 3):
-                finish(k - 3)
-            if is_unit(k - 1):
-                transpose_d(k - 1)
+        for k in range(-1, UNITS + 4):
+            if is_unit(k - 4):
+                finish(k - 4)
+            if is_unit(k + 1):
+                project(k + 1, R_GATE, "r_ps", 2)
+            if is_unit(k):
+                project(k, C_GATE, "c_ps", 1)
+            if is_unit(k + 1):
+                project(k + 1, U_GATE, "u_ps", 2)
             if is_unit(k):
                 sigmoid_gate(k, R_GATE, reset, "reset")
                 candidate_input(k)
-            if is_unit(k + 1):
-                project(k + 1)
             if is_unit(k - 1):
+                transpose_d(k - 1)
                 candidate(k - 1)
                 difference(k - 1)
                 scale_by_update(k - 1)
-            if is_unit(k - 2):
-                transpose_step(k - 2)
+            if is_unit(k - 3):
+                transpose_step(k - 3)
             if is_unit(k):
                 sigmoid_gate(k, U_GATE, update, "update")

@@ -223,7 +223,7 @@ def tile_blockrecurrentmodel_pb_e_kernel(tc, h, d, W_gate_words, W_gate_scales, 
                     )
 
         def finish(k):
-            result = work.tile([P, ROW_TILES, UNIT], F32, bufs=4)
+            result = work.tile([P, ROW_TILES, UNIT], F32, bufs=UNITS)
             nc.vector.tensor_tensor(out=result[:], in0=step_t[k][:], in1=d_unit(k, 0, UNIT), op=ALU.add)
             nc.sync.dma_start(out=out_rows[:, :, k * UNIT : (k + 1) * UNIT], in_=result[:])
 

@@ -30,6 +30,7 @@ GROUPS_PER_H_LOAD = 2
 GROUPS_PER_D_LOAD = 2
 PLANES_PER_TILE = 4
 BIAS_ROWS = GROUPS * GATES * FEATURE_TILES
+BIAS_BEHIND_GROUP = 3
 
 FLOPS = 2 * ROWS * BLOCK * GATES * BLOCK * GROUPS
 
@@ -126,17 +127,17 @@ def tile_blockrecurrentmodel_pb_e_kernel(tc, h, d, W_gate_words, W_gate_scales, 
                     out=grouped[:].bitcast(F32).rearrange("p (n u) -> p n u", u=2),
                     in_=h_t[:].rearrange("p u n -> p n u"),
                 )
+                if g == BIAS_BEHIND_GROUP:
+                    bias_ps = prologue_psum.tile([P, P], BF16)
+                    nc.tensor.transpose(bias_ps[:], bias_rows[:], ident_bf16[:])
+                    nc.vector.tensor_copy(out=bias[:], in_=bias_ps[:])
+                    u_bias = bias[:, 0:BIAS_ROWS].rearrange("p (g c) -> p g c", c=GATES * FEATURE_TILES)[
+                        :, :, U_GATE * FEATURE_TILES : (U_GATE + 1) * FEATURE_TILES
+                    ]
+                    nc.vector.tensor_scalar_add(out=u_bias, in0=u_bias, scalar1=-1.0)
                 nc.vector.quantize_mx(
                     out=h_codes[:, g, :].bitcast(FP8X4), scales=h_scales[:, g, :], in_=grouped[:]
                 )
-
-            bias_ps = prologue_psum.tile([P, P], BF16)
-            nc.tensor.transpose(bias_ps[:], bias_rows[:], ident_bf16[:])
-            nc.vector.tensor_copy(out=bias[:], in_=bias_ps[:])
-            u_bias = bias[:, 0:BIAS_ROWS].rearrange("p (g c) -> p g c", c=GATES * FEATURE_TILES)[
-                :, :, U_GATE * FEATURE_TILES : (U_GATE + 1) * FEATURE_TILES
-            ]
-            nc.vector.tensor_scalar_add(out=u_bias, in0=u_bias, scalar1=-1.0)
 
         psum = ctx.enter_context(tc.psum_pool(name="psum", bufs=1))
         unit_shape = [P, UNIT_TILES, ROWS]

@@ -28,6 +28,8 @@ UNITS_PER_GROUP = BLOCK // UNIT
 UNITS = GROUPS * UNITS_PER_GROUP
 GROUPS_PER_H_LOAD = 2
 GROUPS_PER_D_LOAD = 2
+H_LOADS_BEFORE_W0 = 3
+GROUPS_BEFORE_LOOP = H_LOADS_BEFORE_W0 * GROUPS_PER_H_LOAD
 PLANES_PER_TILE = 4
 BIAS_ROWS = GROUPS * GATES * FEATURE_TILES
 BIAS_BEHIND_GROUP = 3
@@ -61,12 +63,12 @@ def tile_blockrecurrentmodel_pb_e_kernel(tc, h, d, W_gate_words, W_gate_scales, 
         nc.vector.memset(warm[:], 0.0)
         nc.scalar.activation(out=warm[:], in_=warm[:], func=ACT.Sigmoid)
 
-        h_sb = []
-        for c in range(GROUPS // GROUPS_PER_H_LOAD):
+        h_sb = {}
+
+        def load_h(c):
             cols = slice(c * GROUPS_PER_H_LOAD * BLOCK, (c + 1) * GROUPS_PER_H_LOAD * BLOCK)
-            h_chunk = resident.tile([P, ROW_TILES, GROUPS_PER_H_LOAD * BLOCK], BF16, name="h_chunk%d" % c)
-            nc.sync.dma_start(out=h_chunk[:], in_=h_rows[:, :, cols])
-            h_sb.append(h_chunk)
+            h_sb[c] = resident.tile([P, ROW_TILES, GROUPS_PER_H_LOAD * BLOCK], BF16, name="h_chunk%d" % c)
+            nc.sync.dma_start(out=h_sb[c][:], in_=h_rows[:, :, cols])
 
         w_scales = consts.tile([P, GROUPS // PLANES_PER_TILE, GATES * BLOCK], U8, align_bytes=64)
         nc.vector.memset(w_scales[:].rearrange("p a n -> p (a n)").bitcast(I32), 0)
@@ -80,6 +82,8 @@ def tile_blockrecurrentmodel_pb_e_kernel(tc, h, d, W_gate_words, W_gate_scales, 
                     ].bitcast(I32),
                 )
 
+        for c in range(H_LOADS_BEFORE_W0):
+            load_h(c)
         w_words = []
         d_sb = []
         for g in range(GROUPS):
@@ -91,6 +95,9 @@ def tile_blockrecurrentmodel_pb_e_kernel(tc, h, d, W_gate_words, W_gate_scales, 
                 in_=W_gate_words[g].rearrange("p n t -> p (n t)").bitcast(I32),
             )
             w_words.append(words)
+            if g == 0:
+                for c in range(H_LOADS_BEFORE_W0, GROUPS // GROUPS_PER_H_LOAD):
+                    load_h(c)
             if g % GROUPS_PER_D_LOAD == GROUPS_PER_D_LOAD - 1:
                 c = g // GROUPS_PER_D_LOAD
                 cols = slice(c * GROUPS_PER_D_LOAD * BLOCK, (c + 1) * GROUPS_PER_D_LOAD * BLOCK)
@@ -105,28 +112,41 @@ def tile_blockrecurrentmodel_pb_e_kernel(tc, h, d, W_gate_words, W_gate_scales, 
         h_codes = consts.tile([P, GROUPS, ROWS], U32, align_bytes=64)
         h_scales = consts.tile([P, GROUPS, ROWS], U8, align_bytes=64)
         bias = consts.tile([P, P], F32)
+        h_t = {}
+        grouped = {}
 
         def bias_column(g, gate, j):
             column = (g * GATES + gate) * FEATURE_TILES + j
             return bias[:, column : column + 1]
 
+        def transpose_h(g, pool, tag, banks):
+            h_t[g] = pool.tile([P, 2, ROWS], F32, name=tag, tag=tag, bufs=banks)
+            first_word = (g % GROUPS_PER_H_LOAD) * (BLOCK // 2)
+            for m in range(ROW_TILES):
+                h_words = h_sb[g // GROUPS_PER_H_LOAD][:, m, :].bitcast(F32)
+                for u in range(2):
+                    nc.tensor.transpose(
+                        h_t[g][:, u, m * P : (m + 1) * P],
+                        h_words[:, first_word + u : first_word + BLOCK // 2 : 2],
+                        ident_f32[:],
+                    )
+
+        def gather_h(g, copy):
+            grouped[g] = stage.tile([P, ROWS * 4], BF16, name="grouped", tag="grouped", align_bytes=64, bufs=4)
+            copy(
+                out=grouped[g][:].bitcast(F32).rearrange("p (n u) -> p n u", u=2),
+                in_=h_t[g][:].rearrange("p u n -> p n u"),
+            )
+
+        def quantize_h(g):
+            nc.vector.quantize_mx(
+                out=h_codes[:, g, :].bitcast(FP8X4), scales=h_scales[:, g, :], in_=grouped[g][:]
+            )
+
         with tc.psum_pool(name="prologue_psum", bufs=1) as prologue_psum:
-            for g in range(GROUPS):
-                h_t = prologue_psum.tile([P, 2, ROWS], F32, bufs=4)
-                first_word = (g % GROUPS_PER_H_LOAD) * (BLOCK // 2)
-                for m in range(ROW_TILES):
-                    h_words = h_sb[g // GROUPS_PER_H_LOAD][:, m, :].bitcast(F32)
-                    for u in range(2):
-                        nc.tensor.transpose(
-                            h_t[:, u, m * P : (m + 1) * P],
-                            h_words[:, first_word + u : first_word + BLOCK // 2 : 2],
-                            ident_f32[:],
-                        )
-                grouped = stage.tile([P, ROWS * 4], BF16, align_bytes=64, bufs=4)
-                nc.scalar.copy(
-                    out=grouped[:].bitcast(F32).rearrange("p (n u) -> p n u", u=2),
-                    in_=h_t[:].rearrange("p u n -> p n u"),
-                )
+            for g in range(GROUPS_BEFORE_LOOP):
+                transpose_h(g, prologue_psum, "h_t", 4)
+                gather_h(g, nc.scalar.copy)
                 if g == BIAS_BEHIND_GROUP:
                     bias_ps = prologue_psum.tile([P, P], BF16)
                     nc.tensor.transpose(bias_ps[:], bias_rows[:], ident_bf16[:])
@@ -135,9 +155,7 @@ def tile_blockrecurrentmodel_pb_e_kernel(tc, h, d, W_gate_words, W_gate_scales, 
                         :, :, U_GATE * FEATURE_TILES : (U_GATE + 1) * FEATURE_TILES
                     ]
                     nc.vector.tensor_scalar_add(out=u_bias, in0=u_bias, scalar1=-1.0)
-                nc.vector.quantize_mx(
-                    out=h_codes[:, g, :].bitcast(FP8X4), scales=h_scales[:, g, :], in_=grouped[:]
-                )
+                quantize_h(g)
 
         psum = ctx.enter_context(tc.psum_pool(name="psum", bufs=1))
         unit_shape = [P, UNIT_TILES, ROWS]
@@ -201,8 +219,8 @@ def tile_blockrecurrentmodel_pb_e_kernel(tc, h, d, W_gate_words, W_gate_scales, 
         def d_unit(k, first_feature, features):
             return d_block(k // UNITS_PER_GROUP, (k % UNITS_PER_GROUP) * UNIT + first_feature, features)
 
-        def transpose_d(k):
-            d_t[k] = psum.tile(unit_shape, BF16, name="d_t", tag="d_t")
+        def transpose_d(k, tag, banks):
+            d_t[k] = psum.tile(unit_shape, BF16, name=tag, tag=tag, bufs=banks)
             for i in range(UNIT_TILES):
                 for m in range(ROW_TILES):
                     nc.tensor.transpose(d_t[k][:, i, m * P : (m + 1) * P], d_unit(k, i * P, P)[:, m, :], ident_bf16[:])
@@ -211,12 +229,15 @@ def tile_blockrecurrentmodel_pb_e_kernel(tc, h, d, W_gate_words, W_gate_scales, 
             diff[k] = work.tile(unit_shape, F32, name="diff", tag="diff", bufs=2)
             nc.vector.tensor_tensor(out=diff[k][:], in0=cand[k][:], in1=d_t[k][:], op=ALU.subtract)
 
-        def scale_by_update(k):
+        def scale_by_update(k, shares):
             step[k] = work.tile(unit_shape, F32, name="step", tag="step", bufs=3)
-            nc.gpsimd.tensor_tensor(out=step[k][:], in0=diff[k][:], in1=update[k][:], op=ALU.mult)
+            for engine, tiles in shares:
+                engine.tensor_tensor(
+                    out=step[k][:, tiles, :], in0=diff[k][:, tiles, :], in1=update[k][:, tiles, :], op=ALU.mult
+                )
 
-        def transpose_step(k):
-            step_t[k] = psum.tile([P, ROW_TILES, UNIT], F32, name="step_t", tag="step_t", bufs=2)
+        def transpose_step(k, tag, banks):
+            step_t[k] = psum.tile([P, ROW_TILES, UNIT], F32, name=tag, tag=tag, bufs=banks)
             for m in range(ROW_TILES):
                 for i in range(UNIT_TILES):
                     nc.tensor.transpose(
@@ -231,6 +252,7 @@ def tile_blockrecurrentmodel_pb_e_kernel(tc, h, d, W_gate_words, W_gate_scales, 
         def is_unit(k):
             return 0 <= k < UNITS
 
+        whole_unit = slice(0, UNIT_TILES)
         for k in range(-1, UNITS + 4):
             if is_unit(k - 4):
                 finish(k - 4)
@@ -244,11 +266,19 @@ def tile_blockrecurrentmodel_pb_e_kernel(tc, h, d, W_gate_words, W_gate_scales, 
                 sigmoid_gate(k, R_GATE, reset, "reset")
                 candidate_input(k)
             if is_unit(k - 1):
-                transpose_d(k - 1)
+                transpose_d(k - 1, "d_t", 1)
                 candidate(k - 1)
                 difference(k - 1)
-                scale_by_update(k - 1)
+                scale_by_update(k - 1, [(nc.gpsimd, whole_unit)])
+            if k == 0:
+                for g in range(GROUPS_BEFORE_LOOP, GROUPS):
+                    transpose_h(g, psum, "step_t", 2)
             if is_unit(k - 3):
-                transpose_step(k - 3)
+                transpose_step(k - 3, "step_t", 2)
             if is_unit(k):
                 sigmoid_gate(k, U_GATE, update, "update")
+            if k == 0:
+                for g in range(GROUPS_BEFORE_LOOP, GROUPS):
+                    gather_h(g, nc.vector.tensor_copy)
+                for g in range(GROUPS_BEFORE_LOOP, GROUPS):
+                    quantize_h(g)

@@ -26,13 +26,10 @@ UNIT_TILES = 2
 UNIT = UNIT_TILES * P
 UNITS_PER_GROUP = BLOCK // UNIT
 UNITS = GROUPS * UNITS_PER_GROUP
-GROUPS_PER_H_LOAD = 2
-GROUPS_PER_D_LOAD = 2
-H_LOADS_BEFORE_W0 = 3
-GROUPS_BEFORE_LOOP = H_LOADS_BEFORE_W0 * GROUPS_PER_H_LOAD
+TURN_BANKS = 3
+GROUPS_COPIED_BY_VECTOR = 4
 PLANES_PER_TILE = 4
 BIAS_ROWS = GROUPS * GATES * FEATURE_TILES
-BIAS_BEHIND_GROUP = 3
 
 FLOPS = 2 * ROWS * BLOCK * GATES * BLOCK * GROUPS
 
@@ -64,11 +61,20 @@ def tile_blockrecurrentmodel_pb_e_kernel(tc, h, d, W_gate_words, W_gate_scales, 
         nc.scalar.activation(out=warm[:], in_=warm[:], func=ACT.Sigmoid)
 
         h_sb = {}
+        d_sb = {}
+        w_words = {}
 
-        def load_h(c):
-            cols = slice(c * GROUPS_PER_H_LOAD * BLOCK, (c + 1) * GROUPS_PER_H_LOAD * BLOCK)
-            h_sb[c] = resident.tile([P, ROW_TILES, GROUPS_PER_H_LOAD * BLOCK], BF16, name="h_chunk%d" % c)
-            nc.sync.dma_start(out=h_sb[c][:], in_=h_rows[:, :, cols])
+        def load_rows(target, source, name, first, groups):
+            chunk = resident.tile([P, ROW_TILES, groups * BLOCK], BF16, name="%s%d" % (name, first))
+            nc.sync.dma_start(out=chunk[:], in_=source[:, :, first * BLOCK : (first + groups) * BLOCK])
+            for g in range(first, first + groups):
+                target[g] = (chunk, (g - first) * BLOCK)
+
+        def load_h(first, groups):
+            load_rows(h_sb, h_rows, "h", first, groups)
+
+        def load_d(first, groups):
+            load_rows(d_sb, d_rows, "d", first, groups)
 
         w_scales = consts.tile([P, GROUPS // PLANES_PER_TILE, GATES * BLOCK], U8, align_bytes=64)
         nc.vector.memset(w_scales[:].rearrange("p a n -> p (a n)").bitcast(I32), 0)
@@ -82,32 +88,45 @@ def tile_blockrecurrentmodel_pb_e_kernel(tc, h, d, W_gate_words, W_gate_scales, 
                     ].bitcast(I32),
                 )
 
-        for c in range(H_LOADS_BEFORE_W0):
-            load_h(c)
-        w_words = []
-        d_sb = []
-        for g in range(GROUPS):
-            if g % PLANES_PER_TILE == 0:
-                load_scales(g // PLANES_PER_TILE)
-            words = resident.tile([P, GATES * BLOCK], U32, name="w_words%d" % g, align_bytes=64)
+        def load_words(g, first_gate=0, gates=GATES):
+            if g not in w_words:
+                w_words[g] = resident.tile([P, GATES * BLOCK], U32, name="w_words%d" % g, align_bytes=64)
+            cols = slice(first_gate * BLOCK, (first_gate + gates) * BLOCK)
             nc.sync.dma_start(
-                out=words[:].bitcast(I32),
-                in_=W_gate_words[g].rearrange("p n t -> p (n t)").bitcast(I32),
+                out=w_words[g][:, cols].bitcast(I32),
+                in_=W_gate_words[g].rearrange("p n t -> p (n t)").bitcast(I32)[:, cols],
             )
-            w_words.append(words)
-            if g == 0:
-                for c in range(H_LOADS_BEFORE_W0, GROUPS // GROUPS_PER_H_LOAD):
-                    load_h(c)
-            if g % GROUPS_PER_D_LOAD == GROUPS_PER_D_LOAD - 1:
-                c = g // GROUPS_PER_D_LOAD
-                cols = slice(c * GROUPS_PER_D_LOAD * BLOCK, (c + 1) * GROUPS_PER_D_LOAD * BLOCK)
-                d_chunk = resident.tile([P, ROW_TILES, GROUPS_PER_D_LOAD * BLOCK], BF16, name="d_chunk%d" % c)
-                nc.sync.dma_start(out=d_chunk[:], in_=d_rows[:, :, cols])
-                d_sb.append(d_chunk)
+
+        load_h(0, 1)
+        load_scales(0)
+        for gate in (R_GATE, C_GATE, U_GATE):
+            load_words(0, gate, 1)
+        load_h(1, 1)
+        load_words(1)
+        load_d(0, 1)
+        load_h(2, 2)
+        load_words(2)
+        load_d(1, 1)
+        load_words(3)
+        load_h(4, 2)
+        load_d(2, 2)
+        load_scales(1)
+        load_words(4)
+        load_words(5)
+        load_h(6, 2)
+        load_d(4, 2)
+        load_words(6)
+        load_words(7)
+        load_d(6, 2)
 
         def d_block(g, first_feature, features):
-            start = (g % GROUPS_PER_D_LOAD) * BLOCK + first_feature
-            return d_sb[g // GROUPS_PER_D_LOAD][:, :, start : start + features]
+            chunk, start = d_sb[g]
+            return chunk[:, :, start + first_feature : start + first_feature + features]
+
+        psum = ctx.enter_context(tc.psum_pool(name="psum", bufs=1))
+
+        def turn_bank(shape, dtype):
+            return psum.tile(shape, dtype, name="turn", tag="turn", bufs=TURN_BANKS)
 
         h_codes = consts.tile([P, GROUPS, ROWS], U32, align_bytes=64)
         h_scales = consts.tile([P, GROUPS, ROWS], U8, align_bytes=64)
@@ -119,11 +138,12 @@ def tile_blockrecurrentmodel_pb_e_kernel(tc, h, d, W_gate_words, W_gate_scales, 
             column = (g * GATES + gate) * FEATURE_TILES + j
             return bias[:, column : column + 1]
 
-        def transpose_h(g, pool, tag, banks):
-            h_t[g] = pool.tile([P, 2, ROWS], F32, name=tag, tag=tag, bufs=banks)
-            first_word = (g % GROUPS_PER_H_LOAD) * (BLOCK // 2)
+        def transpose_h(g):
+            h_t[g] = turn_bank([P, 2, ROWS], F32)
+            chunk, start = h_sb[g]
+            first_word = start // 2
             for m in range(ROW_TILES):
-                h_words = h_sb[g // GROUPS_PER_H_LOAD][:, m, :].bitcast(F32)
+                h_words = chunk[:, m, :].bitcast(F32)
                 for u in range(2):
                     nc.tensor.transpose(
                         h_t[g][:, u, m * P : (m + 1) * P],
@@ -143,21 +163,15 @@ def tile_blockrecurrentmodel_pb_e_kernel(tc, h, d, W_gate_words, W_gate_scales, 
                 out=h_codes[:, g, :].bitcast(FP8X4), scales=h_scales[:, g, :], in_=grouped[g][:]
             )
 
-        with tc.psum_pool(name="prologue_psum", bufs=1) as prologue_psum:
-            for g in range(GROUPS_BEFORE_LOOP):
-                transpose_h(g, prologue_psum, "h_t", 4)
-                gather_h(g, nc.scalar.copy)
-                if g == BIAS_BEHIND_GROUP:
-                    bias_ps = prologue_psum.tile([P, P], BF16)
-                    nc.tensor.transpose(bias_ps[:], bias_rows[:], ident_bf16[:])
-                    nc.vector.tensor_copy(out=bias[:], in_=bias_ps[:])
-                    u_bias = bias[:, 0:BIAS_ROWS].rearrange("p (g c) -> p g c", c=GATES * FEATURE_TILES)[
-                        :, :, U_GATE * FEATURE_TILES : (U_GATE + 1) * FEATURE_TILES
-                    ]
-                    nc.vector.tensor_scalar_add(out=u_bias, in0=u_bias, scalar1=-1.0)
-                quantize_h(g)
+        def spread_bias():
+            bias_ps = turn_bank([P, P], BF16)
+            nc.tensor.transpose(bias_ps[:], bias_rows[:], ident_bf16[:])
+            nc.vector.tensor_copy(out=bias[:], in_=bias_ps[:])
+            u_bias = bias[:, 0:BIAS_ROWS].rearrange("p (g c) -> p g c", c=GATES * FEATURE_TILES)[
+                :, :, U_GATE * FEATURE_TILES : (U_GATE + 1) * FEATURE_TILES
+            ]
+            nc.vector.tensor_scalar_add(out=u_bias, in0=u_bias, scalar1=-1.0)
 
-        psum = ctx.enter_context(tc.psum_pool(name="psum", bufs=1))
         unit_shape = [P, UNIT_TILES, ROWS]
         gate_ps = {}
         reset = {}
@@ -219,8 +233,8 @@ def tile_blockrecurrentmodel_pb_e_kernel(tc, h, d, W_gate_words, W_gate_scales, 
         def d_unit(k, first_feature, features):
             return d_block(k // UNITS_PER_GROUP, (k % UNITS_PER_GROUP) * UNIT + first_feature, features)
 
-        def transpose_d(k, tag, banks):
-            d_t[k] = psum.tile(unit_shape, BF16, name=tag, tag=tag, bufs=banks)
+        def transpose_d(k):
+            d_t[k] = turn_bank(unit_shape, BF16)
             for i in range(UNIT_TILES):
                 for m in range(ROW_TILES):
                     nc.tensor.transpose(d_t[k][:, i, m * P : (m + 1) * P], d_unit(k, i * P, P)[:, m, :], ident_bf16[:])
@@ -236,8 +250,8 @@ def tile_blockrecurrentmodel_pb_e_kernel(tc, h, d, W_gate_words, W_gate_scales, 
                     out=step[k][:, tiles, :], in0=diff[k][:, tiles, :], in1=update[k][:, tiles, :], op=ALU.mult
                 )
 
-        def transpose_step(k, tag, banks):
-            step_t[k] = psum.tile([P, ROW_TILES, UNIT], F32, name=tag, tag=tag, bufs=banks)
+        def transpose_step(k):
+            step_t[k] = turn_bank([P, ROW_TILES, UNIT], F32)
             for m in range(ROW_TILES):
                 for i in range(UNIT_TILES):
                     nc.tensor.transpose(
@@ -253,32 +267,46 @@ def tile_blockrecurrentmodel_pb_e_kernel(tc, h, d, W_gate_words, W_gate_scales, 
             return 0 <= k < UNITS
 
         whole_unit = slice(0, UNIT_TILES)
+
+        def h_round(g):
+            return max(g * UNITS_PER_GROUP - 3, 0)
+
+        transpose_h(0)
+        gather_h(0, nc.scalar.copy)
+        quantize_h(0)
+        spread_bias()
         for k in range(-1, UNITS + 4):
             if is_unit(k - 4):
                 finish(k - 4)
+            if is_unit(k):
+                project(k, U_GATE, "u_ps", 2)
+                project(k, C_GATE, "c_ps", 1)
             if is_unit(k + 1):
                 project(k + 1, R_GATE, "r_ps", 2)
             if is_unit(k):
-                project(k, C_GATE, "c_ps", 1)
-            if is_unit(k + 1):
-                project(k + 1, U_GATE, "u_ps", 2)
-            if is_unit(k):
                 sigmoid_gate(k, R_GATE, reset, "reset")
+            for g in range(GROUPS_COPIED_BY_VECTOR, GROUPS):
+                if k == h_round(g) + 1:
+                    gather_h(g, nc.scalar.copy)
+            if is_unit(k):
                 candidate_input(k)
+            for g in range(2, GROUPS):
+                if k == h_round(g) + 1:
+                    quantize_h(g)
             if is_unit(k - 1):
-                transpose_d(k - 1, "d_t", 1)
+                transpose_d(k - 1)
                 candidate(k - 1)
                 difference(k - 1)
                 scale_by_update(k - 1, [(nc.gpsimd, whole_unit)])
-            if k == 0:
-                for g in range(GROUPS_BEFORE_LOOP, GROUPS):
-                    transpose_h(g, psum, "step_t", 2)
+            for g in range(1, GROUPS):
+                if k == h_round(g):
+                    transpose_h(g)
             if is_unit(k - 3):
-                transpose_step(k - 3, "step_t", 2)
+                transpose_step(k - 3)
             if is_unit(k):
                 sigmoid_gate(k, U_GATE, update, "update")
-            if k == 0:
-                for g in range(GROUPS_BEFORE_LOOP, GROUPS):
+            for g in range(1, GROUPS_COPIED_BY_VECTOR):
+                if k == h_round(g):
                     gather_h(g, nc.vector.tensor_copy)
-                for g in range(GROUPS_BEFORE_LOOP, GROUPS):
-                    quantize_h(g)
+            if k == h_round(1):
+                quantize_h(1)

@@ -27,6 +27,9 @@ UNIT = UNIT_TILES * P
 UNITS_PER_GROUP = BLOCK // UNIT
 UNITS = GROUPS * UNITS_PER_GROUP
 TURN_BANKS = 3
+LAST = UNITS - 1
+UNITS_FINISHED_BY_SCALAR = (UNITS - 4, UNITS - 3)
+PRODUCTS_BY_VECTOR = 2
 GROUPS_COPIED_BY_VECTOR = 4
 PLANES_PER_TILE = 4
 BIAS_ROWS = GROUPS * GATES * FEATURE_TILES
@@ -52,14 +55,6 @@ def tile_blockrecurrentmodel_pb_e_kernel(tc, h, d, W_gate_words, W_gate_scales, 
         ident_bf16 = consts.tile([P, P], BF16)
         make_identity(nc, ident_bf16[:])
 
-        bias_rows = consts.tile([P, P], BF16)
-        nc.vector.memset(bias_rows[:], 0.0)
-        nc.scalar.dma_start(out=bias_rows[0:BIAS_ROWS, :], in_=b_gate.rearrange("g (c p) -> (g c) p", p=P))
-
-        warm = consts.tile([P, 1], F32)
-        nc.vector.memset(warm[:], 0.0)
-        nc.scalar.activation(out=warm[:], in_=warm[:], func=ACT.Sigmoid)
-
         h_sb = {}
         d_sb = {}
         w_words = {}
@@ -79,9 +74,15 @@ def tile_blockrecurrentmodel_pb_e_kernel(tc, h, d, W_gate_words, W_gate_scales, 
         w_scales = consts.tile([P, GROUPS // PLANES_PER_TILE, GATES * BLOCK], U8, align_bytes=64)
         nc.vector.memset(w_scales[:].rearrange("p a n -> p (a n)").bitcast(I32), 0)
 
-        def load_scales(a):
+        bias_rows = consts.tile([P, P], BF16)
+        nc.vector.memset(bias_rows[:], 0.0)
+
+        def load_bias():
+            nc.sync.dma_start(out=bias_rows[0:BIAS_ROWS, :], in_=b_gate.rearrange("g (c p) -> (g c) p", p=P))
+
+        def load_scales(a, queue):
             for quadrant in range(4):
-                nc.sync.dma_start(
+                queue.dma_start(
                     out=w_scales[32 * quadrant : 32 * quadrant + 16, a, :].bitcast(I32),
                     in_=W_gate_scales[
                         PLANES_PER_TILE * a : PLANES_PER_TILE * (a + 1), 4 * quadrant : 4 * quadrant + 4, :
@@ -98,19 +99,21 @@ def tile_blockrecurrentmodel_pb_e_kernel(tc, h, d, W_gate_words, W_gate_scales, 
             )
 
         load_h(0, 1)
-        load_scales(0)
-        for gate in (R_GATE, C_GATE, U_GATE):
-            load_words(0, gate, 1)
+        load_words(0, R_GATE, 1)
         load_h(1, 1)
+        load_words(0, C_GATE, 1)
+        load_scales(0, nc.scalar)
+        load_bias()
+        load_words(0, U_GATE, 1)
         load_words(1)
         load_d(0, 1)
         load_h(2, 2)
         load_words(2)
         load_d(1, 1)
-        load_words(3)
         load_h(4, 2)
+        load_words(3)
         load_d(2, 2)
-        load_scales(1)
+        load_scales(1, nc.sync)
         load_words(4)
         load_words(5)
         load_h(6, 2)
@@ -118,6 +121,10 @@ def tile_blockrecurrentmodel_pb_e_kernel(tc, h, d, W_gate_words, W_gate_scales, 
         load_words(6)
         load_words(7)
         load_d(6, 2)
+
+        warm = consts.tile([P, 1], F32)
+        nc.vector.memset(warm[:], 0.0)
+        nc.scalar.activation(out=warm[:], in_=warm[:], func=ACT.Sigmoid)
 
         def d_block(g, first_feature, features):
             chunk, start = d_sb[g]
@@ -226,9 +233,15 @@ def tile_blockrecurrentmodel_pb_e_kernel(tc, h, d, W_gate_words, W_gate_scales, 
                     op1=ALU.mult,
                 )
 
+        def row_parts(k):
+            if k == LAST:
+                return [slice(m * P, (m + 1) * P) for m in range(ROW_TILES)]
+            return [slice(0, ROWS)]
+
         def candidate(k):
             cand[k] = work.tile(unit_shape, F32, name="cand", tag="cand", bufs=2)
-            nc.scalar.activation(out=cand[k][:], in_=cand_in[k][:], func=ACT.Tanh)
+            for rows in row_parts(k):
+                nc.scalar.activation(out=cand[k][:, :, rows], in_=cand_in[k][:, :, rows], func=ACT.Tanh)
 
         def d_unit(k, first_feature, features):
             return d_block(k // UNITS_PER_GROUP, (k % UNITS_PER_GROUP) * UNIT + first_feature, features)
@@ -241,32 +254,62 @@ def tile_blockrecurrentmodel_pb_e_kernel(tc, h, d, W_gate_words, W_gate_scales, 
 
         def difference(k):
             diff[k] = work.tile(unit_shape, F32, name="diff", tag="diff", bufs=2)
-            nc.vector.tensor_tensor(out=diff[k][:], in0=cand[k][:], in1=d_t[k][:], op=ALU.subtract)
+            for rows in row_parts(k):
+                nc.vector.tensor_tensor(
+                    out=diff[k][:, :, rows], in0=cand[k][:, :, rows], in1=d_t[k][:, :, rows], op=ALU.subtract
+                )
 
-        def scale_by_update(k, shares):
+        def scale_by_update(k):
             step[k] = work.tile(unit_shape, F32, name="step", tag="step", bufs=3)
-            for engine, tiles in shares:
+            engine = nc.vector if k >= UNITS - PRODUCTS_BY_VECTOR else nc.gpsimd
+            for rows in row_parts(k):
                 engine.tensor_tensor(
-                    out=step[k][:, tiles, :], in0=diff[k][:, tiles, :], in1=update[k][:, tiles, :], op=ALU.mult
+                    out=step[k][:, :, rows], in0=diff[k][:, :, rows], in1=update[k][:, :, rows], op=ALU.mult
                 )
 
         def transpose_step(k):
-            step_t[k] = turn_bank([P, ROW_TILES, UNIT], F32)
+            if k == LAST:
+                step_t[k] = [
+                    turn_bank([P, UNIT], F32),
+                    psum.tile([P, UNIT], F32, name="last_rows", tag="c_ps", bufs=1),
+                ]
+            else:
+                bank = turn_bank([P, ROW_TILES, UNIT], F32)
+                step_t[k] = [bank[:, m, :] for m in range(ROW_TILES)]
+            adds = k in UNITS_FINISHED_BY_SCALAR
+            if adds:
+                nc.tensor.matmul(bank[:], ident_bf16[:], d_unit(k, 0, UNIT), start=True, stop=False)
             for m in range(ROW_TILES):
                 for i in range(UNIT_TILES):
-                    nc.tensor.transpose(
-                        step_t[k][:, m, i * P : (i + 1) * P], step[k][:, i, m * P : (m + 1) * P], ident_f32[:]
+                    nc.tensor.matmul(
+                        step_t[k][m][:, i * P : (i + 1) * P],
+                        step[k][:, i, m * P : (m + 1) * P],
+                        ident_f32[:],
+                        start=not adds,
+                        stop=not adds or (m, i) == (ROW_TILES - 1, UNIT_TILES - 1),
+                        is_transpose=True,
                     )
+            if k != LAST:
+                step_t[k] = bank
 
         def finish(k):
-            result = work.tile([P, ROW_TILES, UNIT], F32, bufs=UNITS)
-            nc.vector.tensor_tensor(out=result[:], in0=step_t[k][:], in1=d_unit(k, 0, UNIT), op=ALU.add)
-            nc.sync.dma_start(out=out_rows[:, :, k * UNIT : (k + 1) * UNIT], in_=result[:])
+            columns = slice(k * UNIT, (k + 1) * UNIT)
+            if k == LAST:
+                for m in range(ROW_TILES):
+                    half = work.tile([P, UNIT], F32, name="half%d" % m, bufs=1)
+                    nc.vector.tensor_tensor(out=half[:], in0=step_t[k][m][:], in1=d_unit(k, 0, UNIT)[:, m, :], op=ALU.add)
+                    nc.sync.dma_start(out=out_rows[:, m, columns], in_=half[:])
+                return
+            result = work.tile([P, ROW_TILES, UNIT], F32, name="result", tag="result", bufs=LAST)
+            if k in UNITS_FINISHED_BY_SCALAR:
+                nc.scalar.copy(out=result[:], in_=step_t[k][:])
+            else:
+                nc.vector.tensor_tensor(out=result[:], in0=step_t[k][:], in1=d_unit(k, 0, UNIT), op=ALU.add)
+            nc.sync.dma_start(out=out_rows[:, :, columns], in_=result[:])
 
         def is_unit(k):
             return 0 <= k < UNITS
 
-        whole_unit = slice(0, UNIT_TILES)
 
         def h_round(g):
             return max(g * UNITS_PER_GROUP - 3, 0)
@@ -276,6 +319,8 @@ def tile_blockrecurrentmodel_pb_e_kernel(tc, h, d, W_gate_words, W_gate_scales, 
         quantize_h(0)
         spread_bias()
         for k in range(-1, UNITS + 4):
+            if is_unit(k):
+                sigmoid_gate(k, R_GATE, reset, "reset")
             if is_unit(k - 4):
                 finish(k - 4)
             if is_unit(k):
@@ -283,8 +328,6 @@ def tile_blockrecurrentmodel_pb_e_kernel(tc, h, d, W_gate_words, W_gate_scales, 
                 project(k, C_GATE, "c_ps", 1)
             if is_unit(k + 1):
                 project(k + 1, R_GATE, "r_ps", 2)
-            if is_unit(k):
-                sigmoid_gate(k, R_GATE, reset, "reset")
             for g in range(GROUPS_COPIED_BY_VECTOR, GROUPS):
                 if k == h_round(g) + 1:
                     gather_h(g, nc.scalar.copy)
@@ -297,16 +340,16 @@ def tile_blockrecurrentmodel_pb_e_kernel(tc, h, d, W_gate_words, W_gate_scales, 
                 transpose_d(k - 1)
                 candidate(k - 1)
                 difference(k - 1)
-                scale_by_update(k - 1, [(nc.gpsimd, whole_unit)])
+                scale_by_update(k - 1)
             for g in range(1, GROUPS):
                 if k == h_round(g):
                     transpose_h(g)
             if is_unit(k - 3):
                 transpose_step(k - 3)
-            if is_unit(k):
-                sigmoid_gate(k, U_GATE, update, "update")
             for g in range(1, GROUPS_COPIED_BY_VECTOR):
                 if k == h_round(g):
                     gather_h(g, nc.vector.tensor_copy)
             if k == h_round(1):
                 quantize_h(1)
+            if is_unit(k):
+                sigmoid_gate(k, U_GATE, update, "update")

@@ -50,6 +50,10 @@ def tile_blockrecurrentmodel_pb_e_kernel(tc, h, d, W_gate_words, W_gate_scales, 
         stage = ctx.enter_context(tc.tile_pool(name="stage", bufs=2))
         work = ctx.enter_context(tc.tile_pool(name="work", bufs=2))
 
+        bias_rows = consts.tile([P, P], BF16)
+        nc.vector.memset(bias_rows[BIAS_ROWS:P, :], 0.0)
+        nc.scalar.dma_start(out=bias_rows[0:BIAS_ROWS, :], in_=b_gate.rearrange("g (c p) -> (g c) p", p=P))
+
         ident_f32 = consts.tile([P, P], F32)
         make_identity(nc, ident_f32[:])
         ident_bf16 = consts.tile([P, P], BF16)
@@ -72,39 +76,26 @@ def tile_blockrecurrentmodel_pb_e_kernel(tc, h, d, W_gate_words, W_gate_scales, 
             load_rows(d_sb, d_rows, "d", first, groups)
 
         w_scales = consts.tile([P, GROUPS // PLANES_PER_TILE, GATES * BLOCK], U8, align_bytes=64)
-        nc.vector.memset(w_scales[:].rearrange("p a n -> p (a n)").bitcast(I32), 0)
+        nc.vector.memset(w_scales[:, 1, :].bitcast(I32), 0)
 
-        bias_rows = consts.tile([P, P], BF16)
-        nc.vector.memset(bias_rows[:], 0.0)
-
-        def load_bias():
-            nc.sync.dma_start(out=bias_rows[0:BIAS_ROWS, :], in_=b_gate.rearrange("g (c p) -> (g c) p", p=P))
-
-        def load_scales(a, queue):
+        def load_scales(block, first, groups, queue):
             for quadrant in range(4):
                 queue.dma_start(
-                    out=w_scales[32 * quadrant : 32 * quadrant + 16, a, :].bitcast(I32),
-                    in_=W_gate_scales[
-                        PLANES_PER_TILE * a : PLANES_PER_TILE * (a + 1), 4 * quadrant : 4 * quadrant + 4, :
-                    ].bitcast(I32),
+                    out=w_scales[32 * quadrant : 32 * quadrant + 4 * groups, block, :].bitcast(I32),
+                    in_=W_gate_scales[first : first + groups, 4 * quadrant : 4 * quadrant + 4, :].bitcast(I32),
                 )
 
-        def load_words(g, first_gate=0, gates=GATES):
-            if g not in w_words:
-                w_words[g] = resident.tile([P, GATES * BLOCK], U32, name="w_words%d" % g, align_bytes=64)
-            cols = slice(first_gate * BLOCK, (first_gate + gates) * BLOCK)
+        def load_words(g):
+            w_words[g] = resident.tile([P, GATES * BLOCK], U32, name="w_words%d" % g, align_bytes=64)
             nc.sync.dma_start(
-                out=w_words[g][:, cols].bitcast(I32),
-                in_=W_gate_words[g].rearrange("p n t -> p (n t)").bitcast(I32)[:, cols],
+                out=w_words[g][:].bitcast(I32),
+                in_=W_gate_words[g].rearrange("p n t -> p (n t)").bitcast(I32),
             )
 
+        load_scales(0, 0, GROUPS, nc.scalar)
         load_h(0, 1)
-        load_words(0, R_GATE, 1)
+        load_words(0)
         load_h(1, 1)
-        load_words(0, C_GATE, 1)
-        load_scales(0, nc.scalar)
-        load_bias()
-        load_words(0, U_GATE, 1)
         load_words(1)
         load_d(0, 1)
         load_h(2, 2)
@@ -113,7 +104,7 @@ def tile_blockrecurrentmodel_pb_e_kernel(tc, h, d, W_gate_words, W_gate_scales, 
         load_h(4, 2)
         load_words(3)
         load_d(2, 2)
-        load_scales(1, nc.sync)
+        load_scales(1, PLANES_PER_TILE, PLANES_PER_TILE, nc.sync)
         load_words(4)
         load_words(5)
         load_h(6, 2)

@@ -29,6 +29,7 @@ UNITS = GROUPS * UNITS_PER_GROUP
 TURN_BANKS = 3
 LAST = UNITS - 1
 UNITS_FINISHED_BY_SCALAR = (UNITS - 4, UNITS - 3)
+UNITS_D_BY_PRODUCT = 4
 PRODUCTS_BY_VECTOR = 2
 GROUPS_COPIED_BY_VECTOR = 4
 PLANES_PER_TILE = 4
@@ -161,6 +162,14 @@ def tile_blockrecurrentmodel_pb_e_kernel(tc, h, d, W_gate_words, W_gate_scales, 
                 out=h_codes[:, g, :].bitcast(FP8X4), scales=h_scales[:, g, :], in_=grouped[g][:]
             )
 
+        zeros = consts.tile([P, BLOCK], BF16)
+        nc.vector.memset(zeros[:], 0.0)
+
+        def warm_up(matmuls):
+            bank = turn_bank([P, BLOCK], F32)
+            for i in range(matmuls):
+                nc.tensor.matmul(bank[:], zeros[:, 0:P], zeros[:], start=True, stop=True)
+
         def spread_bias():
             bias_ps = turn_bank([P, P], BF16)
             nc.tensor.transpose(bias_ps[:], bias_rows[:], ident_bf16[:])
@@ -238,10 +247,15 @@ def tile_blockrecurrentmodel_pb_e_kernel(tc, h, d, W_gate_words, W_gate_scales, 
             return d_block(k // UNITS_PER_GROUP, (k % UNITS_PER_GROUP) * UNIT + first_feature, features)
 
         def transpose_d(k):
-            d_t[k] = turn_bank(unit_shape, BF16)
+            by_product = k < UNITS_D_BY_PRODUCT
+            d_t[k] = turn_bank(unit_shape, F32 if by_product else BF16)
             for i in range(UNIT_TILES):
                 for m in range(ROW_TILES):
-                    nc.tensor.transpose(d_t[k][:, i, m * P : (m + 1) * P], d_unit(k, i * P, P)[:, m, :], ident_bf16[:])
+                    out, d_tile = d_t[k][:, i, m * P : (m + 1) * P], d_unit(k, i * P, P)[:, m, :]
+                    if by_product:
+                        nc.tensor.matmul(out, d_tile, ident_bf16[:], start=True, stop=True)
+                    else:
+                        nc.tensor.transpose(out, d_tile, ident_bf16[:])
 
         def difference(k):
             diff[k] = work.tile(unit_shape, F32, name="diff", tag="diff", bufs=2)
@@ -305,10 +319,12 @@ def tile_blockrecurrentmodel_pb_e_kernel(tc, h, d, W_gate_words, W_gate_scales, 
         def h_round(g):
             return max(g * UNITS_PER_GROUP - 3, 0)
 
+        warm_up(4)
         transpose_h(0)
         gather_h(0, nc.scalar.copy)
         quantize_h(0)
         spread_bias()
+        warm_up(2)
         for k in range(-1, UNITS + 4):
             if is_unit(k):
                 sigmoid_gate(k, R_GATE, reset, "reset")

@@ -53,7 +53,6 @@ def tile_blockrecurrentmodel_pb_e_kernel(tc, h, d, W_gate_words, W_gate_scales, 
 
         bias_rows = consts.tile([P, P], BF16)
         nc.vector.memset(bias_rows[BIAS_ROWS:P, :], 0.0)
-        nc.scalar.dma_start(out=bias_rows[0:BIAS_ROWS, :], in_=b_gate.rearrange("g (c p) -> (g c) p", p=P))
 
         ident_f32 = consts.tile([P, P], F32)
         make_identity(nc, ident_f32[:])
@@ -79,9 +78,12 @@ def tile_blockrecurrentmodel_pb_e_kernel(tc, h, d, W_gate_words, W_gate_scales, 
         w_scales = consts.tile([P, GROUPS // PLANES_PER_TILE, GATES * BLOCK], U8, align_bytes=64)
         nc.vector.memset(w_scales[:, 1, :].bitcast(I32), 0)
 
-        def load_scales(block, first, groups, queue):
+        def load_bias():
+            nc.sync.dma_start(out=bias_rows[0:BIAS_ROWS, :], in_=b_gate.rearrange("g (c p) -> (g c) p", p=P))
+
+        def load_scales(block, first, groups):
             for quadrant in range(4):
-                queue.dma_start(
+                nc.sync.dma_start(
                     out=w_scales[32 * quadrant : 32 * quadrant + 4 * groups, block, :].bitcast(I32),
                     in_=W_gate_scales[first : first + groups, 4 * quadrant : 4 * quadrant + 4, :].bitcast(I32),
                 )
@@ -93,8 +95,9 @@ def tile_blockrecurrentmodel_pb_e_kernel(tc, h, d, W_gate_words, W_gate_scales, 
                 in_=W_gate_words[g].rearrange("p n t -> p (n t)").bitcast(I32),
             )
 
-        load_scales(0, 0, GROUPS, nc.scalar)
         load_h(0, 1)
+        load_scales(0, 0, GROUPS)
+        load_bias()
         load_words(0)
         load_h(1, 1)
         load_words(1)
@@ -105,7 +108,7 @@ def tile_blockrecurrentmodel_pb_e_kernel(tc, h, d, W_gate_words, W_gate_scales, 
         load_h(4, 2)
         load_words(3)
         load_d(2, 2)
-        load_scales(1, PLANES_PER_TILE, PLANES_PER_TILE, nc.sync)
+        load_scales(1, PLANES_PER_TILE, PLANES_PER_TILE)
         load_words(4)
         load_words(5)
         load_h(6, 2)
@@ -319,7 +322,7 @@ def tile_blockrecurrentmodel_pb_e_kernel(tc, h, d, W_gate_words, W_gate_scales, 
         def h_round(g):
             return max(g * UNITS_PER_GROUP - 3, 0)
 
-        warm_up(4)
+        warm_up(3)
         transpose_h(0)
         gather_h(0, nc.scalar.copy)
         quantize_h(0)

@@ -29,7 +29,7 @@ UNITS = GROUPS * UNITS_PER_GROUP
 TURN_BANKS = 3
 LAST = UNITS - 1
 UNITS_FINISHED_BY_SCALAR = (UNITS - 4, UNITS - 3)
-UNITS_D_BY_PRODUCT = 4
+UNITS_D_BY_PRODUCT = 8
 PRODUCTS_BY_VECTOR = 2
 GROUPS_COPIED_BY_VECTOR = 4
 PLANES_PER_TILE = 4
@@ -81,9 +81,9 @@ def tile_blockrecurrentmodel_pb_e_kernel(tc, h, d, W_gate_words, W_gate_scales, 
         def load_bias():
             nc.sync.dma_start(out=bias_rows[0:BIAS_ROWS, :], in_=b_gate.rearrange("g (c p) -> (g c) p", p=P))
 
-        def load_scales(block, first, groups):
+        def load_scales(block, first, groups, queue):
             for quadrant in range(4):
-                nc.sync.dma_start(
+                queue.dma_start(
                     out=w_scales[32 * quadrant : 32 * quadrant + 4 * groups, block, :].bitcast(I32),
                     in_=W_gate_scales[first : first + groups, 4 * quadrant : 4 * quadrant + 4, :].bitcast(I32),
                 )
@@ -96,19 +96,20 @@ def tile_blockrecurrentmodel_pb_e_kernel(tc, h, d, W_gate_words, W_gate_scales, 
             )
 
         load_h(0, 1)
-        load_scales(0, 0, GROUPS)
         load_bias()
         load_words(0)
-        load_h(1, 1)
+        load_h(1, 2)
+        load_scales(0, 0, GROUPS, nc.scalar)
         load_words(1)
         load_d(0, 1)
-        load_h(2, 2)
+        load_h(3, 1)
         load_words(2)
         load_d(1, 1)
-        load_h(4, 2)
         load_words(3)
-        load_d(2, 2)
-        load_scales(1, PLANES_PER_TILE, PLANES_PER_TILE)
+        load_h(4, 2)
+        load_d(2, 1)
+        load_d(3, 1)
+        load_scales(1, PLANES_PER_TILE, PLANES_PER_TILE, nc.sync)
         load_words(4)
         load_words(5)
         load_h(6, 2)

from contextlib import ExitStack

import concourse.mybir as mybir
from concourse.masks import make_identity

F32 = mybir.dt.float32
BF16 = mybir.dt.bfloat16
I32 = mybir.dt.int32
U32 = mybir.dt.uint32
U8 = mybir.dt.uint8
FP8X4 = mybir.dt.float8_e4m3fn_x4
ACT = mybir.ActivationFunctionType
ALU = mybir.AluOpType

P = 128
ROWS = 256
ROW_TILES = ROWS // P
GROUPS = 8
BLOCK = 512
GATES = 3
R_GATE = 0
U_GATE = 1
C_GATE = 2
FEATURE_TILES = BLOCK // P
UNIT_TILES = 2
UNIT = UNIT_TILES * P
UNITS_PER_GROUP = BLOCK // UNIT
UNITS = GROUPS * UNITS_PER_GROUP
TURN_BANKS = 3
LAST = UNITS - 1
UNITS_FINISHED_BY_SCALAR = (UNITS - 4, UNITS - 3)
UNITS_D_BY_PRODUCT = 8
PRODUCTS_BY_VECTOR = 2
GROUPS_COPIED_BY_VECTOR = 4
PLANES_PER_TILE = 4
BIAS_ROWS = GROUPS * GATES * FEATURE_TILES

FLOPS = 2 * ROWS * BLOCK * GATES * BLOCK * GROUPS


def tile_blockrecurrentmodel_pb_e_kernel(tc, h, d, W_gate_words, W_gate_scales, b_gate, out):
    nc = tc.nc
    h_rows = h.rearrange("(m p) k -> p m k", p=P)
    d_rows = d.rearrange("b t k -> (b t) k").rearrange("(m p) k -> p m k", p=P)
    out_rows = out.rearrange("b t k -> (b t) k").rearrange("(m p) k -> p m k", p=P)

    with ExitStack() as ctx:
        ctx.enter_context(tc.manual_schedule())
        consts = ctx.enter_context(tc.tile_pool(name="consts", bufs=1))
        resident = ctx.enter_context(tc.tile_pool(name="resident", bufs=1))
        stage = ctx.enter_context(tc.tile_pool(name="stage", bufs=2))
        work = ctx.enter_context(tc.tile_pool(name="work", bufs=2))

        bias_rows = consts.tile([P, P], BF16)
        nc.vector.memset(bias_rows[BIAS_ROWS:P, :], 0.0)

        ident_f32 = consts.tile([P, P], F32)
        make_identity(nc, ident_f32[:])
        ident_bf16 = consts.tile([P, P], BF16)
        make_identity(nc, ident_bf16[:])

        h_sb = {}
        d_sb = {}
        w_words = {}

        def load_rows(target, source, name, first, groups):
            chunk = resident.tile([P, ROW_TILES, groups * BLOCK], BF16, name="%s%d" % (name, first))
            nc.sync.dma_start(out=chunk[:], in_=source[:, :, first * BLOCK : (first + groups) * BLOCK])
            for g in range(first, first + groups):
                target[g] = (chunk, (g - first) * BLOCK)

        def load_h(first, groups):
            load_rows(h_sb, h_rows, "h", first, groups)

        def load_d(first, groups):
            load_rows(d_sb, d_rows, "d", first, groups)

        w_scales = consts.tile([P, GROUPS // PLANES_PER_TILE, GATES * BLOCK], U8, align_bytes=64)
        nc.vector.memset(w_scales[:, 1, :].bitcast(I32), 0)

        def load_bias():
            nc.sync.dma_start(out=bias_rows[0:BIAS_ROWS, :], in_=b_gate.rearrange("g (c p) -> (g c) p", p=P))

        def load_scales(block, first, groups, queue):
            for quadrant in range(4):
                queue.dma_start(
                    out=w_scales[32 * quadrant : 32 * quadrant + 4 * groups, block, :].bitcast(I32),
                    in_=W_gate_scales[first : first + groups, 4 * quadrant : 4 * quadrant + 4, :].bitcast(I32),
                )

        def load_words(g):
            w_words[g] = resident.tile([P, GATES * BLOCK], U32, name="w_words%d" % g, align_bytes=64)
            nc.sync.dma_start(
                out=w_words[g][:].bitcast(I32),
                in_=W_gate_words[g].rearrange("p n t -> p (n t)").bitcast(I32),
            )

        load_h(0, 1)
        load_bias()
        load_words(0)
        load_h(1, 2)
        load_scales(0, 0, GROUPS, nc.scalar)
        load_words(1)
        load_d(0, 1)
        load_h(3, 1)
        load_words(2)
        load_d(1, 1)
        load_words(3)
        load_h(4, 2)
        load_d(2, 1)
        load_d(3, 1)
        load_scales(1, PLANES_PER_TILE, PLANES_PER_TILE, nc.sync)
        load_words(4)
        load_words(5)
        load_h(6, 2)
        load_d(4, 2)
        load_words(6)
        load_words(7)
        load_d(6, 2)

        warm = consts.tile([P, 1], F32)
        nc.vector.memset(warm[:], 0.0)
        nc.scalar.activation(out=warm[:], in_=warm[:], func=ACT.Sigmoid)

        def d_block(g, first_feature, features):
            chunk, start = d_sb[g]
            return chunk[:, :, start + first_feature : start + first_feature + features]

        psum = ctx.enter_context(tc.psum_pool(name="psum", bufs=1))

        def turn_bank(shape, dtype):
            return psum.tile(shape, dtype, name="turn", tag="turn", bufs=TURN_BANKS)

        h_codes = consts.tile([P, GROUPS, ROWS], U32, align_bytes=64)
        h_scales = consts.tile([P, GROUPS, ROWS], U8, align_bytes=64)
        bias = consts.tile([P, P], F32)
        h_t = {}
        grouped = {}

        def bias_column(g, gate, j):
            column = (g * GATES + gate) * FEATURE_TILES + j
            return bias[:, column : column + 1]

        def transpose_h(g):
            h_t[g] = turn_bank([P, 2, ROWS], F32)
            chunk, start = h_sb[g]
            first_word = start // 2
            for m in range(ROW_TILES):
                h_words = chunk[:, m, :].bitcast(F32)
                for u in range(2):
                    nc.tensor.transpose(
                        h_t[g][:, u, m * P : (m + 1) * P],
                        h_words[:, first_word + u : first_word + BLOCK // 2 : 2],
                        ident_f32[:],
                    )

        def gather_h(g, copy):
            grouped[g] = stage.tile([P, ROWS * 4], BF16, name="grouped", tag="grouped", align_bytes=64, bufs=4)
            copy(
                out=grouped[g][:].bitcast(F32).rearrange("p (n u) -> p n u", u=2),
                in_=h_t[g][:].rearrange("p u n -> p n u"),
            )

        def quantize_h(g):
            nc.vector.quantize_mx(
                out=h_codes[:, g, :].bitcast(FP8X4), scales=h_scales[:, g, :], in_=grouped[g][:]
            )

        zeros = consts.tile([P, BLOCK], BF16)
        nc.vector.memset(zeros[:], 0.0)

        def warm_up(matmuls):
            bank = turn_bank([P, BLOCK], F32)
            for i in range(matmuls):
                nc.tensor.matmul(bank[:], zeros[:, 0:P], zeros[:], start=True, stop=True)

        def spread_bias():
            bias_ps = turn_bank([P, P], BF16)
            nc.tensor.transpose(bias_ps[:], bias_rows[:], ident_bf16[:])
            nc.vector.tensor_copy(out=bias[:], in_=bias_ps[:])
            u_bias = bias[:, 0:BIAS_ROWS].rearrange("p (g c) -> p g c", c=GATES * FEATURE_TILES)[
                :, :, U_GATE * FEATURE_TILES : (U_GATE + 1) * FEATURE_TILES
            ]
            nc.vector.tensor_scalar_add(out=u_bias, in0=u_bias, scalar1=-1.0)

        unit_shape = [P, UNIT_TILES, ROWS]
        gate_ps = {}
        reset = {}
        update = {}
        cand_in = {}
        cand = {}
        d_t = {}
        diff = {}
        step = {}
        step_t = {}

        def project(k, gate, tag, banks):
            g = k // UNITS_PER_GROUP
            offset = 4 * (g % PLANES_PER_TILE)
            bank = psum.tile(unit_shape, F32, name=tag, tag=tag, bufs=banks)
            gate_ps[(k, gate)] = bank
            for i in range(UNIT_TILES):
                first = gate * BLOCK + (k % UNITS_PER_GROUP) * UNIT + i * P
                nc.tensor.matmul_mx(
                    out=bank[:, i, :],
                    lhsT=w_words[g][:, first : first + P].bitcast(FP8X4),
                    lhsT_scale=w_scales[offset:P, g // PLANES_PER_TILE, first : first + P],
                    rhs=h_codes[:, g, :].bitcast(FP8X4),
                    rhs_scale=h_scales[:, g, :],
                    start=True,
                    stop=True,
                )

        def unit_bias(k, gate, i):
            return bias_column(k // UNITS_PER_GROUP, gate, (k % UNITS_PER_GROUP) * UNIT_TILES + i)

        def sigmoid_gate(k, gate, target, tag):
            target[k] = work.tile(unit_shape, F32, name=tag, tag=tag, bufs=3)
            for i in range(UNIT_TILES):
                nc.scalar.activation(
                    out=target[k][:, i, :],
                    in_=gate_ps[(k, gate)][:, i, :],
                    func=ACT.Sigmoid,
                    bias=unit_bias(k, gate, i),
                    scale=1.0,
                )

        def candidate_input(k):
            cand_in[k] = work.tile(unit_shape, F32, name="cand_in", tag="cand_in", bufs=3)
            for i in range(UNIT_TILES):
                nc.vector.scalar_tensor_tensor(
                    out=cand_in[k][:, i, :],
                    in0=gate_ps[(k, C_GATE)][:, i, :],
                    scalar=unit_bias(k, C_GATE, i),
                    in1=reset[k][:, i, :],
                    op0=ALU.add,
                    op1=ALU.mult,
                )

        def row_parts(k):
            if k == LAST:
                return [slice(m * P, (m + 1) * P) for m in range(ROW_TILES)]
            return [slice(0, ROWS)]

        def candidate(k):
            cand[k] = work.tile(unit_shape, F32, name="cand", tag="cand", bufs=2)
            for rows in row_parts(k):
                nc.scalar.activation(out=cand[k][:, :, rows], in_=cand_in[k][:, :, rows], func=ACT.Tanh)

        def d_unit(k, first_feature, features):
            return d_block(k // UNITS_PER_GROUP, (k % UNITS_PER_GROUP) * UNIT + first_feature, features)

        def transpose_d(k):
            by_product = k < UNITS_D_BY_PRODUCT
            d_t[k] = turn_bank(unit_shape, F32 if by_product else BF16)
            for i in range(UNIT_TILES):
                for m in range(ROW_TILES):
                    out, d_tile = d_t[k][:, i, m * P : (m + 1) * P], d_unit(k, i * P, P)[:, m, :]
                    if by_product:
                        nc.tensor.matmul(out, d_tile, ident_bf16[:], start=True, stop=True)
                    else:
                        nc.tensor.transpose(out, d_tile, ident_bf16[:])

        def difference(k):
            diff[k] = work.tile(unit_shape, F32, name="diff", tag="diff", bufs=2)
            for rows in row_parts(k):
                nc.vector.tensor_tensor(
                    out=diff[k][:, :, rows], in0=cand[k][:, :, rows], in1=d_t[k][:, :, rows], op=ALU.subtract
                )

        def scale_by_update(k):
            step[k] = work.tile(unit_shape, F32, name="step", tag="step", bufs=3)
            engine = nc.vector if k >= UNITS - PRODUCTS_BY_VECTOR else nc.gpsimd
            for rows in row_parts(k):
                engine.tensor_tensor(
                    out=step[k][:, :, rows], in0=diff[k][:, :, rows], in1=update[k][:, :, rows], op=ALU.mult
                )

        def transpose_step(k):
            if k == LAST:
                step_t[k] = [
                    turn_bank([P, UNIT], F32),
                    psum.tile([P, UNIT], F32, name="last_rows", tag="c_ps", bufs=1),
                ]
            else:
                bank = turn_bank([P, ROW_TILES, UNIT], F32)
                step_t[k] = [bank[:, m, :] for m in range(ROW_TILES)]
            adds = k in UNITS_FINISHED_BY_SCALAR
            if adds:
                nc.tensor.matmul(bank[:], ident_bf16[:], d_unit(k, 0, UNIT), start=True, stop=False)
            for m in range(ROW_TILES):
                for i in range(UNIT_TILES):
                    nc.tensor.matmul(
                        step_t[k][m][:, i * P : (i + 1) * P],
                        step[k][:, i, m * P : (m + 1) * P],
                        ident_f32[:],
                        start=not adds,
                        stop=not adds or (m, i) == (ROW_TILES - 1, UNIT_TILES - 1),
                        is_transpose=True,
                    )
            if k != LAST:
                step_t[k] = bank

        def finish(k):
            columns = slice(k * UNIT, (k + 1) * UNIT)
            if k == LAST:
                for m in range(ROW_TILES):
                    half = work.tile([P, UNIT], F32, name="half%d" % m, bufs=1)
                    nc.vector.tensor_tensor(out=half[:], in0=step_t[k][m][:], in1=d_unit(k, 0, UNIT)[:, m, :], op=ALU.add)
                    nc.sync.dma_start(out=out_rows[:, m, columns], in_=half[:])
                return
            result = work.tile([P, ROW_TILES, UNIT], F32, name="result", tag="result", bufs=LAST)
            if k in UNITS_FINISHED_BY_SCALAR:
                nc.scalar.copy(out=result[:], in_=step_t[k][:])
            else:
                nc.vector.tensor_tensor(out=result[:], in0=step_t[k][:], in1=d_unit(k, 0, UNIT), op=ALU.add)
            nc.sync.dma_start(out=out_rows[:, :, columns], in_=result[:])

        def is_unit(k):
            return 0 <= k < UNITS


        def h_round(g):
            return max(g * UNITS_PER_GROUP - 3, 0)

        warm_up(3)
        transpose_h(0)
        gather_h(0, nc.scalar.copy)
        quantize_h(0)
        spread_bias()
        warm_up(2)
        for k in range(-1, UNITS + 4):
            if is_unit(k):
                sigmoid_gate(k, R_GATE, reset, "reset")
            if is_unit(k - 4):
                finish(k - 4)
            if is_unit(k):
                project(k, U_GATE, "u_ps", 2)
                project(k, C_GATE, "c_ps", 1)
            if is_unit(k + 1):
                project(k + 1, R_GATE, "r_ps", 2)
            for g in range(GROUPS_COPIED_BY_VECTOR, GROUPS):
                if k == h_round(g) + 1:
                    gather_h(g, nc.scalar.copy)
            if is_unit(k):
                candidate_input(k)
            for g in range(2, GROUPS):
                if k == h_round(g) + 1:
                    quantize_h(g)
            if is_unit(k - 1):
                transpose_d(k - 1)
                candidate(k - 1)
                difference(k - 1)
                scale_by_update(k - 1)
            for g in range(1, GROUPS):
                if k == h_round(g):
                    transpose_h(g)
            if is_unit(k - 3):
                transpose_step(k - 3)
            for g in range(1, GROUPS_COPIED_BY_VECTOR):
                if k == h_round(g):
                    gather_h(g, nc.vector.tensor_copy)
            if k == h_round(1):
                quantize_h(1)
            if is_unit(k):
                sigmoid_gate(k, U_GATE, update, "update")
